import numpy as np
import ml_dtypes


def mxq(x, axis, fmt="e4m3"):
    dtype, down = {"e4m3": (ml_dtypes.float8_e4m3fn, 7), "e5m2": (ml_dtypes.float8_e5m2, 14)}[fmt]
    v = np.moveaxis(np.asarray(x, np.float32).astype(ml_dtypes.bfloat16).astype(np.float64), axis, -1)
    blocks = v.reshape(v.shape[:-1] + (-1, 32))
    amax = np.abs(blocks).max(-1, keepdims=True)
    byte = np.maximum(np.where(amax > 0, np.frexp(amax)[1] - 1 + 127, 0) - down, 1)
    scale = np.exp2(byte - 127.0)
    codes = (blocks / scale).astype(np.float32).astype(dtype).astype(np.float64)
    return np.moveaxis((codes * scale).reshape(v.shape), -1, axis)


WIDE = False


def mx_kscale(k):
    if not WIDE:
        return np.ones(k)
    levels = np.array([10, -10, 5, -5, 0])
    a = np.random.permutation(np.resize(levels, k // 512 * 4)).reshape(k // 512, 4)
    idx = np.arange(k)
    return np.exp2(a[idx // 512, idx % 128 // 32])


BF16 = ml_dtypes.bfloat16


def bf(x):
    return np.asarray(x, np.float32).astype(BF16)


def f64(x):
    return np.asarray(x).astype(np.float64)


E2M1 = np.array([0.0, 0.5, 1.0, 1.5, 2.0, 3.0, 4.0, 6.0, -0.0, -0.5, -1.0, -1.5, -2.0, -3.0, -4.0, -6.0])


def pack_weight(w, fmt):
    k, n = w.shape
    w = f64(bf(w)).reshape(k // 32, 32, n)
    amax = np.abs(w).max(1)
    if fmt == "e4m3":
        byte = np.frexp(amax)[1] - 1 + 127 - 7
    else:
        mant, ex = np.frexp(amax / 6.0)
        byte = np.where(mant > 0.5, ex, ex - 1) + 127
    byte = np.clip(np.where(amax > 0, byte, 1), 1, 254)
    scaled = (w * np.exp2(127.0 - byte)[:, None, :]).reshape(k, n).astype(np.float32)
    by_word = np.ascontiguousarray(scaled.reshape(k // 512, 128, 4, n).transpose(0, 1, 3, 2))
    if fmt == "e4m3":
        words = by_word.astype(ml_dtypes.float8_e4m3fn).view(np.uint8)
    else:
        c = by_word.astype(ml_dtypes.float4_e2m1fn).view(np.uint8) & 0xF
        words = c[..., 0::2] | (c[..., 1::2] << 4)
    return np.ascontiguousarray(words), np.ascontiguousarray(byte.astype(np.uint8).reshape(k // 512, 16, n))


def unpack_weight(words, scales, fmt):
    g, p, n, _ = words.shape
    if fmt == "e4m3":
        vals = np.ascontiguousarray(words).view(ml_dtypes.float8_e4m3fn).astype(np.float64)
    else:
        nib = np.empty((g, p, n, 4), np.uint8)
        nib[..., 0::2] = words & 0xF
        nib[..., 1::2] = words >> 4
        vals = E2M1[nib]
    vals = vals * np.repeat(np.exp2(scales.astype(np.float64) - 127.0), 8, axis=1)[..., None]
    return vals.transpose(0, 1, 3, 2).reshape(g * 512, n)

def pack4(w):
    words, scales = pack_weight(w, "e2m1")
    return words.reshape(words.shape[0], 128, -1), scales


def unpack4(words, scales):
    return unpack_weight(words.reshape(words.shape[0], 128, -1, 2), scales, "e2m1")


B, K, D, H1, H2, C = 2048, 2, 1024, 256, 512, 64
N = B * K


def setup_inputs():
    s = mx_kscale(D)
    nf1 = bf(np.random.standard_normal((N, D)) * s)
    nf2 = bf(np.random.standard_normal((N * K, D)) * s)
    w1_0_words, w1_0_scales = pack4(np.random.standard_normal((D, H1)) / np.sqrt(D) / s[:, None])
    w2_0_words, w2_0_scales = pack4(np.random.standard_normal((D, H1)) / np.sqrt(D) / s[:, None])
    return {"nf1": nf1,
            "nf2": nf2,
            "w1_0_words": w1_0_words,
            "w1_0_scales": w1_0_scales,
            "w2_0_words": w2_0_words,
            "w2_0_scales": w2_0_scales}


def sage_gcn(cur, neigh, w1, w2):
    b, d = cur.shape
    agg = neigh.reshape(b, -1, d).mean(axis=1)
    return np.maximum((mxq(cur, 1, "e4m3") @ w2) + (mxq(agg, 1, "e4m3") @ w1), 0.0)


def reference(nf1, nf2, w1_0_words, w1_0_scales, w2_0_words, w2_0_scales):
    return sage_gcn(f64(nf1), f64(nf2), unpack4(w1_0_words, w1_0_scales), unpack4(w2_0_words, w2_0_scales))

@@ -1,0 +1,196 @@
+from contextlib import ExitStack
+
+import concourse.mybir as mybir
+from concourse.masks import make_identity
+
+F32 = mybir.dt.float32
+BF16 = mybir.dt.bfloat16
+I32 = mybir.dt.int32
+U32 = mybir.dt.uint32
+U8 = mybir.dt.uint8
+FP8X4 = mybir.dt.float8_e4m3fn_x4
+FP4X4 = mybir.dt.float4_e2m1fn_x4
+
+P = 128
+PACK = 4
+K_PASS = P * PACK
+NODES = 4096
+D = 1024
+H = 256
+TILES = NODES // P
+GROUPS = D // K_PASS
+PASSES = 2 * GROUPS
+WORDS = D // 2
+N_HALF = 128
+
+LOAD_TILES = 2
+LOAD_BUFS = 4
+CHUNKS = TILES // LOAD_TILES
+
+FLOPS = 2 * 2 * NODES * D * H
+
+
+def tile_graphsage_pa_t_kernel(
+    tc, nf1, nf2, w1_0_words, w1_0_scales, w2_0_words, w2_0_scales, out
+):
+    nc = tc.nc
+    own_hbm = nf1.rearrange("(p t) k -> p t k", t=TILES)
+    nbr_hbm = nf2.rearrange("(p t b) k -> p t (b k)", t=TILES, b=2)
+    out_hbm = out.rearrange("(p t) h -> p t h", t=TILES)
+
+    with ExitStack() as ctx:
+        consts = ctx.enter_context(tc.tile_pool(name="consts", bufs=1))
+        own_pool = ctx.enter_context(tc.tile_pool(name="own", bufs=LOAD_BUFS))
+        nbr_pool = ctx.enter_context(tc.tile_pool(name="nbr", bufs=LOAD_BUFS))
+        work = ctx.enter_context(tc.tile_pool(name="work", bufs=3))
+        res_pool = ctx.enter_context(tc.tile_pool(name="res", bufs=6))
+        turned_pool = ctx.enter_context(tc.psum_pool(name="turned", bufs=3))
+        acc_pool = ctx.enter_context(tc.psum_pool(name="acc", bufs=2))
+        ctx.enter_context(tc.manual_schedule())
+
+        ident = consts.tile([P, P], F32)
+        make_identity(nc, ident[:])
+        w_words = consts.tile([P, PASSES, 2 * H], U8, align_bytes=64)
+        w_scales = consts.tile([P, PASSES, H], U8, align_bytes=64)
+        nc.vector.memset(w_scales[:].bitcast(I32), 0)
+
+        def load_words(first_pass, words):
+            nc.sync.dma_start(
+                out=w_words[:, first_pass : first_pass + GROUPS, :].bitcast(I32),
+                in_=words.bitcast(I32).rearrange("g p b -> p g b"),
+            )
+
+        def load_scales(first_pass, scales):
+            rows = scales.bitcast(I32).rearrange("g q n -> q g n")
+            for quad in range(4):
+                nc.sync.dma_start(
+                    out=w_scales[
+                        32 * quad : 32 * quad + 4, first_pass : first_pass + GROUPS, :
+                    ].bitcast(I32),
+                    in_=rows[4 * quad : 4 * quad + 4],
+                )
+
+        own_of = {}
+        nbr_of = {}
+
+        def load_chunk(c):
+            tiles = slice(c * LOAD_TILES, (c + 1) * LOAD_TILES)
+            nbr = nbr_pool.tile([P, LOAD_TILES, 2 * D], BF16)
+            nc.sync.dma_start(out=nbr[:], in_=nbr_hbm[:, tiles, :])
+            own = own_pool.tile([P, LOAD_TILES, D], BF16)
+            nc.sync.dma_start(out=own[:], in_=own_hbm[:, tiles, :])
+            nbr_of[c] = nbr
+            own_of[c] = own
+
+        load_words(0, w2_0_words)
+        load_words(GROUPS, w1_0_words)
+        load_scales(0, w2_0_scales)
+        load_chunk(0)
+        load_scales(GROUPS, w1_0_scales)
+        for c in range(1, LOAD_BUFS):
+            load_chunk(c)
+
+        mean_of = {}
+        grouped_of = {}
+        codes_of = {}
+        acc_of = {}
+
+        def mean_sum(t):
+            nbr = nbr_of[t // LOAD_TILES]
+            j = t % LOAD_TILES
+            mean = work.tile([P, D], BF16)
+            nc.vector.tensor_tensor(
+                out=mean[:].rearrange("n (u q e) -> n q u e", u=2, e=2),
+                in0=nbr[:, j, 0:D].rearrange("n (q u e) -> n q u e", u=2, e=2),
+                in1=nbr[:, j, D : 2 * D].rearrange("n (q u e) -> n q u e", u=2, e=2),
+                op=mybir.AluOpType.add,
+            )
+            mean_of[t] = mean
+
+        def mean_halve(t):
+            mean = mean_of[t]
+            nc.vector.tensor_scalar_mul(out=mean[:], in0=mean[:], scalar1=0.5)
+
+        def transpose_and_regroup(t):
+            own_words = own_of[t // LOAD_TILES][:, t % LOAD_TILES, :].bitcast(F32)
+            mean_words = mean_of[t][:].bitcast(F32)
+            own_turned = turned_pool.tile([P, WORDS], F32)
+            mean_turned = turned_pool.tile([P, WORDS], F32)
+            for u in range(2):
+                for g in range(GROUPS):
+                    block = slice((u * GROUPS + g) * P, (u * GROUPS + g + 1) * P)
+                    nc.tensor.transpose(
+                        out=own_turned[:, block],
+                        in_=own_words[:, 2 * P * g + u : 2 * P * (g + 1) : 2],
+                        identity=ident[:],
+                    )
+            for u in range(2):
+                for g in range(GROUPS):
+                    block = slice((u * GROUPS + g) * P, (u * GROUPS + g + 1) * P)
+                    nc.tensor.transpose(
+                        out=mean_turned[:, block], in_=mean_words[:, block], identity=ident[:]
+                    )
+            grouped = work.tile([P, PASSES * P * PACK], BF16, align_bytes=64)
+            for o, turned in enumerate((own_turned, mean_turned)):
+                nc.scalar.copy(
+                    out=grouped[:, o * 2 * WORDS : (o + 1) * 2 * WORDS]
+                    .bitcast(F32)
+                    .rearrange("p (q u) -> p q u", u=2),
+                    in_=turned[:].rearrange("p (u q) -> p q u", u=2),
+                )
+            grouped_of[t] = grouped
+
+        def quantise(t):
+            codes = work.tile([P, PASSES * P], U32, align_bytes=64)
+            scales = work.tile([P, PASSES * P], U8, align_bytes=64)
+            nc.vector.quantize_mx(
+                out=codes[:].bitcast(FP8X4), scales=scales[:], in_=grouped_of[t][:]
+            )
+            codes_of[t] = (codes, scales)
+
+        def multiply(t):
+            if t % 2 == 0:
+                acc = acc_pool.tile([P, 2, H], F32)
+                acc_of[t // 2] = acc
+            acc = acc_of[t // 2]
+            codes, scales = codes_of[t]
+            for half in range(H // N_HALF):
+                for c in range(PASSES):
+                    nodes = slice(c * P, (c + 1) * P)
+                    nc.tensor.matmul_mx(
+                        out=acc[:, t % 2, half * N_HALF : (half + 1) * N_HALF],
+                        lhsT=codes[:, nodes].bitcast(FP8X4),
+                        lhsT_scale=scales[:, nodes],
+                        rhs=w_words[:, c, half * 2 * N_HALF : (half + 1) * 2 * N_HALF].bitcast(
+                            FP4X4
+                        ),
+                        rhs_scale=w_scales[:, c, half * N_HALF : (half + 1) * N_HALF],
+                        start=(c == 0),
+                        stop=(c == PASSES - 1),
+                    )
+
+        def relu_and_store(pair):
+            res = res_pool.tile([P, 2, H], F32)
+            nc.scalar.activation(
+                out=res[:], in_=acc_of[pair][:], func=mybir.ActivationFunctionType.Relu
+            )
+            nc.sync.dma_start(out=out_hbm[:, 2 * pair : 2 * pair + 2, :], in_=res[:])
+
+        mean_sum(0)
+        mean_halve(0)
+        for step in range(TILES + 2):
+            if step + 1 < TILES:
+                mean_sum(step + 1)
+            if step < TILES:
+                transpose_and_regroup(step)
+                c = step // LOAD_TILES
+                if step % LOAD_TILES == LOAD_TILES - 1 and c + LOAD_BUFS < CHUNKS:
+                    load_chunk(c + LOAD_BUFS)
+            if 1 <= step <= TILES:
+                quantise(step - 1)
+            if step + 1 < TILES:
+                mean_halve(step + 1)
+            if step >= 2:
+                multiply(step - 2)
+                if step % 2 == 1:
+                    relu_and_store((step - 2) // 2)

@@ -24,7 +24,8 @@ WORDS = D // 2
 N_HALF = 128
 
 LOAD_TILES = 2
-LOAD_BUFS = 4
+LOAD_BUFS = 8
+STORE_TILES = 4
 CHUNKS = TILES // LOAD_TILES
 
 FLOPS = 2 * 2 * NODES * D * H
@@ -43,7 +44,6 @@ def tile_graphsage_pa_t_kernel(
         own_pool = ctx.enter_context(tc.tile_pool(name="own", bufs=LOAD_BUFS))
         nbr_pool = ctx.enter_context(tc.tile_pool(name="nbr", bufs=LOAD_BUFS))
         work = ctx.enter_context(tc.tile_pool(name="work", bufs=3))
-        res_pool = ctx.enter_context(tc.tile_pool(name="res", bufs=6))
         turned_pool = ctx.enter_context(tc.psum_pool(name="turned", bufs=3))
         acc_pool = ctx.enter_context(tc.psum_pool(name="acc", bufs=2))
         ctx.enter_context(tc.manual_schedule())
@@ -94,6 +94,7 @@ def tile_graphsage_pa_t_kernel(
         grouped_of = {}
         codes_of = {}
         acc_of = {}
+        res = consts.tile([P, TILES, H], F32)
 
         def mean_sum(t):
             nbr = nbr_of[t // LOAD_TILES]
@@ -169,12 +170,12 @@ def tile_graphsage_pa_t_kernel(
                         stop=(c == PASSES - 1),
                     )
 
-        def relu_and_store(pair):
-            res = res_pool.tile([P, 2, H], F32)
+        def relu(pair):
             nc.scalar.activation(
-                out=res[:], in_=acc_of[pair][:], func=mybir.ActivationFunctionType.Relu
+                out=res[:, 2 * pair : 2 * pair + 2, :],
+                in_=acc_of[pair][:],
+                func=mybir.ActivationFunctionType.Relu,
             )
-            nc.sync.dma_start(out=out_hbm[:, 2 * pair : 2 * pair + 2, :], in_=res[:])
 
         mean_sum(0)
         mean_halve(0)
@@ -193,4 +194,7 @@ def tile_graphsage_pa_t_kernel(
             if step >= 2:
                 multiply(step - 2)
                 if step % 2 == 1:
-                    relu_and_store((step - 2) // 2)
+                    relu((step - 2) // 2)
+        for first in range(0, TILES, STORE_TILES):
+            tiles = slice(first, first + STORE_TILES)
+            nc.sync.dma_start(out=out_hbm[:, tiles, :], in_=res[:, tiles, :])

@@ -25,7 +25,8 @@ N_HALF = 128
 
 LOAD_TILES = 2
 LOAD_BUFS = 8
-STORE_TILES = 4
+STORES = [4] * 7 + [2, 1, 1]
+assert sum(STORES) == TILES
 CHUNKS = TILES // LOAD_TILES
 
 FLOPS = 2 * 2 * NODES * D * H
@@ -150,16 +151,18 @@ def tile_graphsage_pa_t_kernel(
             codes_of[t] = (codes, scales)
 
         def multiply(t):
-            if t % 2 == 0:
+            if t % 2 == 0 or t == TILES - 1:
                 acc = acc_pool.tile([P, 2, H], F32)
-                acc_of[t // 2] = acc
-            acc = acc_of[t // 2]
+                acc_of[t] = (acc, 0)
+            else:
+                acc_of[t] = (acc_of[t - 1][0], 1)
+            acc, place = acc_of[t]
             codes, scales = codes_of[t]
             for half in range(H // N_HALF):
                 for c in range(PASSES):
                     nodes = slice(c * P, (c + 1) * P)
                     nc.tensor.matmul_mx(
-                        out=acc[:, t % 2, half * N_HALF : (half + 1) * N_HALF],
+                        out=acc[:, place, half * N_HALF : (half + 1) * N_HALF],
                         lhsT=codes[:, nodes].bitcast(FP8X4),
                         lhsT_scale=scales[:, nodes],
                         rhs=w_words[:, c, half * 2 * N_HALF : (half + 1) * 2 * N_HALF].bitcast(
@@ -170,12 +173,20 @@ def tile_graphsage_pa_t_kernel(
                         stop=(c == PASSES - 1),
                     )
 
-        def relu(pair):
+        def relu(first, count):
+            acc, place = acc_of[first]
             nc.scalar.activation(
-                out=res[:, 2 * pair : 2 * pair + 2, :],
-                in_=acc_of[pair][:],
+                out=res[:, first : first + count, :],
+                in_=acc[:, place : place + count, :],
                 func=mybir.ActivationFunctionType.Relu,
             )
+
+        def finish(t):
+            multiply(t)
+            if t >= TILES - 2:
+                relu(t, 1)
+            elif t % 2 == 1:
+                relu(t - 1, 2)
 
         mean_sum(0)
         mean_halve(0)
@@ -191,10 +202,12 @@ def tile_graphsage_pa_t_kernel(
                 quantise(step - 1)
             if step + 1 < TILES:
                 mean_halve(step + 1)
-            if step >= 2:
-                multiply(step - 2)
-                if step % 2 == 1:
-                    relu((step - 2) // 2)
-        for first in range(0, TILES, STORE_TILES):
-            tiles = slice(first, first + STORE_TILES)
+            if step == TILES - 1:
+                finish(step - 3)
+            if step >= 2 and step != TILES - 2:
+                finish(step - 2)
+        first = 0
+        for count in STORES:
+            tiles = slice(first, first + count)
             nc.sync.dma_start(out=out_hbm[:, tiles, :], in_=res[:, tiles, :])
+            first += count

@@ -102,9 +102,9 @@ def tile_graphsage_pa_t_kernel(
             j = t % LOAD_TILES
             mean = work.tile([P, D], BF16)
             nc.vector.tensor_tensor(
-                out=mean[:].rearrange("n (u q e) -> n q u e", u=2, e=2),
-                in0=nbr[:, j, 0:D].rearrange("n (q u e) -> n q u e", u=2, e=2),
-                in1=nbr[:, j, D : 2 * D].rearrange("n (q u e) -> n q u e", u=2, e=2),
+                out=mean[:].rearrange("n (u q e) -> n u q e", u=2, e=2),
+                in0=nbr[:, j, 0:D].rearrange("n (q u e) -> n u q e", u=2, e=2),
+                in1=nbr[:, j, D : 2 * D].rearrange("n (q u e) -> n u q e", u=2, e=2),
                 op=mybir.AluOpType.add,
             )
             mean_of[t] = mean

@@ -28,6 +28,7 @@ LOAD_BUFS = 8
 STORES = [4] * 7 + [2, 1, 1]
 assert sum(STORES) == TILES
 CHUNKS = TILES // LOAD_TILES
+DMA_ALIGN = 256
 
 FLOPS = 2 * 2 * NODES * D * H
 
@@ -76,9 +77,9 @@ def tile_graphsage_pa_t_kernel(
 
         def load_chunk(c):
             tiles = slice(c * LOAD_TILES, (c + 1) * LOAD_TILES)
-            nbr = nbr_pool.tile([P, LOAD_TILES, 2 * D], BF16)
+            nbr = nbr_pool.tile([P, LOAD_TILES, 2 * D], BF16, align_bytes=DMA_ALIGN)
             nc.sync.dma_start(out=nbr[:], in_=nbr_hbm[:, tiles, :])
-            own = own_pool.tile([P, LOAD_TILES, D], BF16)
+            own = own_pool.tile([P, LOAD_TILES, D], BF16, align_bytes=DMA_ALIGN)
             nc.sync.dma_start(out=own[:], in_=own_hbm[:, tiles, :])
             nbr_of[c] = nbr
             own_of[c] = own
@@ -95,7 +96,7 @@ def tile_graphsage_pa_t_kernel(
         grouped_of = {}
         codes_of = {}
         acc_of = {}
-        res = consts.tile([P, TILES, H], F32)
+        res = consts.tile([P, TILES, H], F32, align_bytes=DMA_ALIGN)
 
         def mean_sum(t):
             nbr = nbr_of[t // LOAD_TILES]

@@ -192,16 +192,21 @@ def tile_graphsage_pa_t_kernel(
         mean_sum(0)
         mean_halve(0)
         for step in range(TILES + 2):
-            if step + 1 < TILES:
+            if step + 1 < TILES - 1:
                 mean_sum(step + 1)
+            if step == TILES - 3:
+                mean_sum(TILES - 1)
             if step < TILES:
                 transpose_and_regroup(step)
                 c = step // LOAD_TILES
                 if step % LOAD_TILES == LOAD_TILES - 1 and c + LOAD_BUFS < CHUNKS:
                     load_chunk(c + LOAD_BUFS)
+            if step == TILES - 3:
+                mean_halve(TILES - 2)
+                mean_halve(TILES - 1)
             if 1 <= step <= TILES:
                 quantise(step - 1)
-            if step + 1 < TILES:
+            if step + 1 < TILES - 2:
                 mean_halve(step + 1)
             if step == TILES - 1:
                 finish(step - 3)

@@ -86,10 +86,11 @@ def tile_graphsage_pa_t_kernel(
 
         load_words(0, w2_0_words)
         load_words(GROUPS, w1_0_words)
-        load_scales(0, w2_0_scales)
         load_chunk(0)
+        load_scales(0, w2_0_scales)
+        load_chunk(1)
         load_scales(GROUPS, w1_0_scales)
-        for c in range(1, LOAD_BUFS):
+        for c in range(2, LOAD_BUFS):
             load_chunk(c)
 
         mean_of = {}

@@ -25,7 +25,7 @@ N_HALF = 128
 
 LOAD_TILES = 2
 LOAD_BUFS = 8
-STORES = [4] * 7 + [2, 1, 1]
+STORES = [16, 8, 4, 2, 1, 1]
 assert sum(STORES) == TILES
 CHUNKS = TILES // LOAD_TILES
 DMA_ALIGN = 256

@@ -25,7 +25,7 @@ N_HALF = 128
 
 LOAD_TILES = 2
 LOAD_BUFS = 8
-STORES = [16, 8, 4, 2, 1, 1]
+STORES = [24, 6, 1, 1]
 assert sum(STORES) == TILES
 CHUNKS = TILES // LOAD_TILES
 DMA_ALIGN = 256

from contextlib import ExitStack

import concourse.mybir as mybir
from concourse.masks import make_identity

F32 = mybir.dt.float32
BF16 = mybir.dt.bfloat16
I32 = mybir.dt.int32
U32 = mybir.dt.uint32
U8 = mybir.dt.uint8
FP8X4 = mybir.dt.float8_e4m3fn_x4
FP4X4 = mybir.dt.float4_e2m1fn_x4

P = 128
PACK = 4
K_PASS = P * PACK
NODES = 4096
D = 1024
H = 256
TILES = NODES // P
GROUPS = D // K_PASS
PASSES = 2 * GROUPS
WORDS = D // 2
N_HALF = 128

LOAD_TILES = 2
LOAD_BUFS = 8
STORES = [24, 6, 1, 1]
assert sum(STORES) == TILES
CHUNKS = TILES // LOAD_TILES
DMA_ALIGN = 256

FLOPS = 2 * 2 * NODES * D * H


def tile_graphsage_pa_t_kernel(
    tc, nf1, nf2, w1_0_words, w1_0_scales, w2_0_words, w2_0_scales, out
):
    nc = tc.nc
    own_hbm = nf1.rearrange("(p t) k -> p t k", t=TILES)
    nbr_hbm = nf2.rearrange("(p t b) k -> p t (b k)", t=TILES, b=2)
    out_hbm = out.rearrange("(p t) h -> p t h", t=TILES)

    with ExitStack() as ctx:
        consts = ctx.enter_context(tc.tile_pool(name="consts", bufs=1))
        own_pool = ctx.enter_context(tc.tile_pool(name="own", bufs=LOAD_BUFS))
        nbr_pool = ctx.enter_context(tc.tile_pool(name="nbr", bufs=LOAD_BUFS))
        work = ctx.enter_context(tc.tile_pool(name="work", bufs=3))
        turned_pool = ctx.enter_context(tc.psum_pool(name="turned", bufs=3))
        acc_pool = ctx.enter_context(tc.psum_pool(name="acc", bufs=2))
        ctx.enter_context(tc.manual_schedule())

        ident = consts.tile([P, P], F32)
        make_identity(nc, ident[:])
        w_words = consts.tile([P, PASSES, 2 * H], U8, align_bytes=64)
        w_scales = consts.tile([P, PASSES, H], U8, align_bytes=64)
        nc.vector.memset(w_scales[:].bitcast(I32), 0)

        def load_words(first_pass, words):
            nc.sync.dma_start(
                out=w_words[:, first_pass : first_pass + GROUPS, :].bitcast(I32),
                in_=words.bitcast(I32).rearrange("g p b -> p g b"),
            )

        def load_scales(first_pass, scales):
            rows = scales.bitcast(I32).rearrange("g q n -> q g n")
            for quad in range(4):
                nc.sync.dma_start(
                    out=w_scales[
                        32 * quad : 32 * quad + 4, first_pass : first_pass + GROUPS, :
                    ].bitcast(I32),
                    in_=rows[4 * quad : 4 * quad + 4],
                )

        own_of = {}
        nbr_of = {}

        def load_chunk(c):
            tiles = slice(c * LOAD_TILES, (c + 1) * LOAD_TILES)
            nbr = nbr_pool.tile([P, LOAD_TILES, 2 * D], BF16, align_bytes=DMA_ALIGN)
            nc.sync.dma_start(out=nbr[:], in_=nbr_hbm[:, tiles, :])
            own = own_pool.tile([P, LOAD_TILES, D], BF16, align_bytes=DMA_ALIGN)
            nc.sync.dma_start(out=own[:], in_=own_hbm[:, tiles, :])
            nbr_of[c] = nbr
            own_of[c] = own

        load_words(0, w2_0_words)
        load_words(GROUPS, w1_0_words)
        load_chunk(0)
        load_scales(0, w2_0_scales)
        load_chunk(1)
        load_scales(GROUPS, w1_0_scales)
        for c in range(2, LOAD_BUFS):
            load_chunk(c)

        mean_of = {}
        grouped_of = {}
        codes_of = {}
        acc_of = {}
        res = consts.tile([P, TILES, H], F32, align_bytes=DMA_ALIGN)

        def mean_sum(t):
            nbr = nbr_of[t // LOAD_TILES]
            j = t % LOAD_TILES
            mean = work.tile([P, D], BF16)
            nc.vector.tensor_tensor(
                out=mean[:].rearrange("n (u q e) -> n u q e", u=2, e=2),
                in0=nbr[:, j, 0:D].rearrange("n (q u e) -> n u q e", u=2, e=2),
                in1=nbr[:, j, D : 2 * D].rearrange("n (q u e) -> n u q e", u=2, e=2),
                op=mybir.AluOpType.add,
            )
            mean_of[t] = mean

        def mean_halve(t):
            mean = mean_of[t]
            nc.vector.tensor_scalar_mul(out=mean[:], in0=mean[:], scalar1=0.5)

        def transpose_and_regroup(t):
            own_words = own_of[t // LOAD_TILES][:, t % LOAD_TILES, :].bitcast(F32)
            mean_words = mean_of[t][:].bitcast(F32)
            own_turned = turned_pool.tile([P, WORDS], F32)
            mean_turned = turned_pool.tile([P, WORDS], F32)
            for u in range(2):
                for g in range(GROUPS):
                    block = slice((u * GROUPS + g) * P, (u * GROUPS + g + 1) * P)
                    nc.tensor.transpose(
                        out=own_turned[:, block],
                        in_=own_words[:, 2 * P * g + u : 2 * P * (g + 1) : 2],
                        identity=ident[:],
                    )
            for u in range(2):
                for g in range(GROUPS):
                    block = slice((u * GROUPS + g) * P, (u * GROUPS + g + 1) * P)
                    nc.tensor.transpose(
                        out=mean_turned[:, block], in_=mean_words[:, block], identity=ident[:]
                    )
            grouped = work.tile([P, PASSES * P * PACK], BF16, align_bytes=64)
            for o, turned in enumerate((own_turned, mean_turned)):
                nc.scalar.copy(
                    out=grouped[:, o * 2 * WORDS : (o + 1) * 2 * WORDS]
                    .bitcast(F32)
                    .rearrange("p (q u) -> p q u", u=2),
                    in_=turned[:].rearrange("p (u q) -> p q u", u=2),
                )
            grouped_of[t] = grouped

        def quantise(t):
            codes = work.tile([P, PASSES * P], U32, align_bytes=64)
            scales = work.tile([P, PASSES * P], U8, align_bytes=64)
            nc.vector.quantize_mx(
                out=codes[:].bitcast(FP8X4), scales=scales[:], in_=grouped_of[t][:]
            )
            codes_of[t] = (codes, scales)

        def multiply(t):
            if t % 2 == 0 or t == TILES - 1:
                acc = acc_pool.tile([P, 2, H], F32)
                acc_of[t] = (acc, 0)
            else:
                acc_of[t] = (acc_of[t - 1][0], 1)
            acc, place = acc_of[t]
            codes, scales = codes_of[t]
            for half in range(H // N_HALF):
                for c in range(PASSES):
                    nodes = slice(c * P, (c + 1) * P)
                    nc.tensor.matmul_mx(
                        out=acc[:, place, half * N_HALF : (half + 1) * N_HALF],
                        lhsT=codes[:, nodes].bitcast(FP8X4),
                        lhsT_scale=scales[:, nodes],
                        rhs=w_words[:, c, half * 2 * N_HALF : (half + 1) * 2 * N_HALF].bitcast(
                            FP4X4
                        ),
                        rhs_scale=w_scales[:, c, half * N_HALF : (half + 1) * N_HALF],
                        start=(c == 0),
                        stop=(c == PASSES - 1),
                    )

        def relu(first, count):
            acc, place = acc_of[first]
            nc.scalar.activation(
                out=res[:, first : first + count, :],
                in_=acc[:, place : place + count, :],
                func=mybir.ActivationFunctionType.Relu,
            )

        def finish(t):
            multiply(t)
            if t >= TILES - 2:
                relu(t, 1)
            elif t % 2 == 1:
                relu(t - 1, 2)

        mean_sum(0)
        mean_halve(0)
        for step in range(TILES + 2):
            if step + 1 < TILES - 1:
                mean_sum(step + 1)
            if step == TILES - 3:
                mean_sum(TILES - 1)
            if step < TILES:
                transpose_and_regroup(step)
                c = step // LOAD_TILES
                if step % LOAD_TILES == LOAD_TILES - 1 and c + LOAD_BUFS < CHUNKS:
                    load_chunk(c + LOAD_BUFS)
            if step == TILES - 3:
                mean_halve(TILES - 2)
                mean_halve(TILES - 1)
            if 1 <= step <= TILES:
                quantise(step - 1)
            if step + 1 < TILES - 2:
                mean_halve(step + 1)
            if step == TILES - 1:
                finish(step - 3)
            if step >= 2 and step != TILES - 2:
                finish(step - 2)
        first = 0
        for count in STORES:
            tiles = slice(first, first + count)
            nc.sync.dma_start(out=out_hbm[:, tiles, :], in_=res[:, tiles, :])
            first += count
